import numpy as np
import ml_dtypes


def mxq(x, axis, fmt="e4m3"):
    dtype, down = {"e4m3": (ml_dtypes.float8_e4m3fn, 7), "e5m2": (ml_dtypes.float8_e5m2, 14)}[fmt]
    v = np.moveaxis(np.asarray(x, np.float32).astype(ml_dtypes.bfloat16).astype(np.float64), axis, -1)
    blocks = v.reshape(v.shape[:-1] + (-1, 32))
    amax = np.abs(blocks).max(-1, keepdims=True)
    byte = np.maximum(np.where(amax > 0, np.frexp(amax)[1] - 1 + 127, 0) - down, 1)
    scale = np.exp2(byte - 127.0)
    codes = (blocks / scale).astype(np.float32).astype(dtype).astype(np.float64)
    return np.moveaxis((codes * scale).reshape(v.shape), -1, axis)


WIDE = False


def mx_kscale(k):
    if not WIDE:
        return np.ones(k)
    levels = np.array([10, -10, 5, -5, 0])
    a = np.random.permutation(np.resize(levels, k // 512 * 4)).reshape(k // 512, 4)
    idx = np.arange(k)
    return np.exp2(a[idx // 512, idx % 128 // 32])


BF16 = ml_dtypes.bfloat16


def bf(x):
    return np.asarray(x, np.float32).astype(BF16)


def f64(x):
    return np.asarray(x).astype(np.float64)


E2M1 = np.array([0.0, 0.5, 1.0, 1.5, 2.0, 3.0, 4.0, 6.0, -0.0, -0.5, -1.0, -1.5, -2.0, -3.0, -4.0, -6.0])


def pack_weight(w, fmt):
    k, n = w.shape
    w = f64(bf(w)).reshape(k // 32, 32, n)
    amax = np.abs(w).max(1)
    if fmt == "e4m3":
        byte = np.frexp(amax)[1] - 1 + 127 - 7
    else:
        mant, ex = np.frexp(amax / 6.0)
        byte = np.where(mant > 0.5, ex, ex - 1) + 127
    byte = np.clip(np.where(amax > 0, byte, 1), 1, 254)
    scaled = (w * np.exp2(127.0 - byte)[:, None, :]).reshape(k, n).astype(np.float32)
    by_word = np.ascontiguousarray(scaled.reshape(k // 512, 128, 4, n).transpose(0, 1, 3, 2))
    if fmt == "e4m3":
        words = by_word.astype(ml_dtypes.float8_e4m3fn).view(np.uint8)
    else:
        c = by_word.astype(ml_dtypes.float4_e2m1fn).view(np.uint8) & 0xF
        words = c[..., 0::2] | (c[..., 1::2] << 4)
    return np.ascontiguousarray(words), np.ascontiguousarray(byte.astype(np.uint8).reshape(k // 512, 16, n))


def unpack_weight(words, scales, fmt):
    g, p, n, _ = words.shape
    if fmt == "e4m3":
        vals = np.ascontiguousarray(words).view(ml_dtypes.float8_e4m3fn).astype(np.float64)
    else:
        nib = np.empty((g, p, n, 4), np.uint8)
        nib[..., 0::2] = words & 0xF
        nib[..., 1::2] = words >> 4
        vals = E2M1[nib]
    vals = vals * np.repeat(np.exp2(scales.astype(np.float64) - 127.0), 8, axis=1)[..., None]
    return vals.transpose(0, 1, 3, 2).reshape(g * 512, n)


B, HEAD, NUM_EXPERTS, HEAD_DIM = 4096, 1, 3, 512
EPS = 1e-5
VAR0 = 3e-4


def setup_inputs():
    s = mx_kscale(HEAD_DIM)
    p = (HEAD, NUM_EXPERTS, HEAD_DIM)

    def draw_x():
        return bf((np.random.standard_normal((B, HEAD, HEAD_DIM)) * s).reshape(B, HEAD * HEAD_DIM))

    x1 = draw_x()
    x2 = draw_x()
    x3 = draw_x()
    W = np.random.standard_normal((HEAD, NUM_EXPERTS, HEAD_DIM, HEAD_DIM)) / np.sqrt(HEAD_DIM) / s
    cat = np.ascontiguousarray(np.swapaxes(W, -1, -2)).reshape(-1, HEAD_DIM)
    words, scales = pack_weight(cat, "e4m3")
    return {"x1": x1, "x2": x2, "x3": x3,
            "W_words": words, "W_scales": scales,
            "b": bf(np.random.standard_normal(p) * 0.3),
            "gamma": bf(np.sqrt(VAR0) * (1.0 + 0.1 * np.random.standard_normal(p))),
            "beta": bf(np.random.standard_normal(p) * 0.3),
            "running_mean": bf(np.random.standard_normal(p) * 0.3),
            "running_var": bf(VAR0 * np.random.uniform(0.5, 1.5, p))}


def reference(x1, x2, x3, W_words, W_scales, b, gamma, beta, running_mean, running_var):
    n = x1.shape[0]
    xs = np.stack([f64(x1).reshape(n, HEAD, HEAD_DIM),
                   f64(x2).reshape(n, HEAD, HEAD_DIM),
                   f64(x3).reshape(n, HEAD, HEAD_DIM)], axis=2)
    xq = mxq(xs, 3, "e4m3")
    wt = unpack_weight(W_words, W_scales, "e4m3").reshape(HEAD, NUM_EXPERTS, HEAD_DIM, HEAD_DIM)
    y = (xq.transpose(1, 2, 0, 3) @ wt).transpose(2, 0, 1, 3) + f64(b)
    y = y * (1.0 / (1.0 + np.exp(-1.702 * y)))
    y = (y - f64(running_mean)) * (1.0 / np.sqrt(f64(running_var) + EPS)) * f64(gamma) + f64(beta)
    return np.transpose(y, (0, 2, 1, 3)).reshape(n, NUM_EXPERTS * HEAD * HEAD_DIM)

@@ -1,0 +1,208 @@
+import concourse.mybir as mybir
+from concourse.masks import make_identity
+
+F32 = mybir.dt.float32
+BF16 = mybir.dt.bfloat16
+I32 = mybir.dt.int32
+U32 = mybir.dt.uint32
+U8 = mybir.dt.uint8
+FP8X4 = mybir.dt.float8_e4m3fn_x4
+ACT = mybir.ActivationFunctionType
+ALU = mybir.AluOpType
+
+P = 128
+ROWS = 4096
+K = 512
+FEATURES = 512
+EXPERTS = 3
+EPS = 1e-5
+
+CHUNK = 512
+ROW_BLOCKS = CHUNK // P
+FEATURE_BLOCKS = FEATURES // P
+CHUNKS = ROWS // CHUNK
+ROUNDS = CHUNKS * EXPERTS
+WORDS = K // 2
+VECTORS = 5
+COLUMNS = EXPERTS * FEATURE_BLOCKS
+
+FLOPS = 2 * ROWS * K * FEATURES * EXPERTS
+
+
+def tile_mom_t_e_kernel(
+    tc, x1, x2, x3, W_words, W_scales, b, gamma, beta, running_mean, running_var, out
+):
+    nc = tc.nc
+    xs = [x1, x2, x3]
+
+    with tc.tile_pool(name="keep", bufs=1) as keep, tc.tile_pool(
+        name="rows_in", bufs=1
+    ) as rows_in, tc.tile_pool(name="quantised", bufs=2) as quantised, tc.tile_pool(
+        name="features_first", bufs=2 * FEATURE_BLOCKS
+    ) as features_first, tc.tile_pool(name="rows_out", bufs=3) as rows_out, tc.psum_pool(
+        name="psum_in", bufs=2
+    ) as psum_in, tc.psum_pool(name="psum_acc", bufs=3) as psum_acc, tc.psum_pool(
+        name="psum_out", bufs=3
+    ) as psum_out, tc.manual_schedule():
+        x_rows = []
+        for r in range(ROUNDS):
+            x_rows.append(rows_in.tile([P, ROW_BLOCKS, K], BF16, name="x_rows%d" % r))
+
+        def load_rows(r):
+            chunk, e = divmod(r, EXPERTS)
+            nc.sync.dma_start(
+                out=x_rows[r][:],
+                in_=xs[e][chunk * CHUNK : (chunk + 1) * CHUNK, :].rearrange(
+                    "(p j) k -> p j k", j=ROW_BLOCKS
+                ),
+            )
+
+        w_scales = keep.tile([P, EXPERTS, FEATURES], U8, align_bytes=64)
+        nc.vector.memset(w_scales[:].rearrange("p g n -> p (g n)").bitcast(I32), 0)
+        load_rows(0)
+        for quadrant in range(4):
+            nc.sync.dma_start(
+                out=w_scales[32 * quadrant : 32 * quadrant + 4, :, :].bitcast(I32),
+                in_=W_scales[:, 4 * quadrant : 4 * quadrant + 4, :]
+                .rearrange("g r n -> r g n")
+                .bitcast(I32),
+            )
+        w_codes = keep.tile([P, EXPERTS, FEATURES], U32, align_bytes=64)
+        for e in range(EXPERTS):
+            nc.sync.dma_start(
+                out=w_codes[:, e, :].bitcast(I32),
+                in_=W_words[e].rearrange("p n t -> p (n t)").bitcast(I32),
+            )
+            load_rows(e + 1)
+        for r in range(EXPERTS + 1, ROUNDS):
+            load_rows(r)
+
+        ident = keep.tile([P, P], F32)
+        make_identity(nc, ident[:])
+        vec_rows = keep.tile([P, P], BF16)
+        nc.vector.memset(vec_rows[:], 0.0)
+        for v, vec in enumerate([b, gamma, beta, running_mean, running_var]):
+            nc.scalar.dma_start(
+                out=vec_rows[v * COLUMNS : (v + 1) * COLUMNS, :],
+                in_=vec.rearrange("o e (c f) -> (o e c) f", f=P),
+            )
+        vec_cols = keep.tile([P, VECTORS, COLUMNS], F32)
+        bias = vec_cols[:, 0, :]
+        gain = keep.tile([P, COLUMNS], F32)
+        shift = keep.tile([P, COLUMNS], F32)
+
+        def spread_vectors():
+            vec_rows_f32 = keep.tile([P, P], F32)
+            nc.vector.tensor_copy(out=vec_rows_f32[:], in_=vec_rows[:])
+            vec_psum = psum_in.tile([P, P], F32, tag="x_psum")
+            nc.tensor.transpose(vec_psum[:], vec_rows_f32[:], ident[:])
+            nc.vector.tensor_copy(
+                out=vec_cols[:].rearrange("p v c -> p (v c)"),
+                in_=vec_psum[:, : VECTORS * COLUMNS],
+            )
+            nc.vector.tensor_scalar_add(out=gain[:], in0=vec_cols[:, 4, :], scalar1=EPS)
+            nc.scalar.sqrt(out=gain[:], in_=gain[:])
+            nc.vector.reciprocal(out=gain[:], in_=gain[:])
+            nc.vector.tensor_mul(out=gain[:], in0=gain[:], in1=vec_cols[:, 1, :])
+            nc.vector.tensor_mul(out=shift[:], in0=gain[:], in1=vec_cols[:, 3, :])
+            nc.vector.tensor_sub(out=shift[:], in0=vec_cols[:, 2, :], in1=shift[:])
+
+        grouped = {}
+        x_codes = {}
+        x_scales = {}
+        finished = {}
+        out_rows = {}
+
+        def transpose_in(r):
+            words = x_rows[r][:].rearrange("p j k -> p (j k)").bitcast(F32)
+            grouped[r] = quantised.tile([P, CHUNK * 4], BF16, name="grouped", align_bytes=64)
+            pairs = grouped[r][:].bitcast(F32).rearrange("p (n u) -> p n u", u=2)
+            for half in range(2):
+                x_psum = psum_in.tile([P, 2, CHUNK // 2], F32, tag="x_psum")
+                for jj in range(ROW_BLOCKS // 2):
+                    j = half * (ROW_BLOCKS // 2) + jj
+                    for u in range(2):
+                        nc.tensor.transpose(
+                            x_psum[:, u, jj * P : (jj + 1) * P],
+                            words[:, j * WORDS + u : (j + 1) * WORDS : 2],
+                            ident[:],
+                        )
+                nc.vector.tensor_copy(
+                    out=pairs[:, half * (CHUNK // 2) : (half + 1) * (CHUNK // 2), :],
+                    in_=x_psum[:].rearrange("p u n -> p n u"),
+                )
+
+        def quantise(r):
+            x_codes[r] = quantised.tile([P, CHUNK], U32, name="x_codes", align_bytes=64)
+            x_scales[r] = quantised.tile([P, CHUNK], U8, name="x_scales", align_bytes=64)
+            nc.vector.quantize_mx(
+                out=x_codes[r][:].bitcast(FP8X4), scales=x_scales[r][:], in_=grouped[r][:]
+            )
+
+        def multiply(r):
+            e = r % EXPERTS
+            for c in range(FEATURE_BLOCKS):
+                cols = slice(c * P, (c + 1) * P)
+                col = slice(e * FEATURE_BLOCKS + c, e * FEATURE_BLOCKS + c + 1)
+                acc = psum_acc.tile([P, CHUNK], F32, name="acc")
+                nc.tensor.matmul_mx(
+                    out=acc[:],
+                    lhsT=w_codes[:, e, cols].bitcast(FP8X4),
+                    lhsT_scale=w_scales[:, e, cols],
+                    rhs=x_codes[r][:].bitcast(FP8X4),
+                    rhs_scale=x_scales[r][:],
+                    start=True,
+                    stop=True,
+                )
+                z = features_first.tile([P, CHUNK], F32, name="z")
+                nc.scalar.activation(
+                    out=z[:], in_=acc[:], func=ACT.Gelu_apprx_sigmoid, bias=bias[:, col], scale=1.0
+                )
+                nc.vector.tensor_scalar(
+                    out=z[:],
+                    in0=z[:],
+                    scalar1=gain[:, col],
+                    scalar2=shift[:, col],
+                    op0=ALU.mult,
+                    op1=ALU.add,
+                )
+                finished[(r, c)] = z
+
+        def transpose_out(r):
+            chunk, e = divmod(r, EXPERTS)
+            if e == 0:
+                out_rows[chunk] = rows_out.tile(
+                    [P, ROW_BLOCKS, EXPERTS * FEATURES], F32, name="out_rows"
+                )
+            for c in range(FEATURE_BLOCKS):
+                o_psum = psum_out.tile([P, ROW_BLOCKS, P], F32, name="o_psum")
+                for j in range(ROW_BLOCKS):
+                    nc.tensor.transpose(
+                        o_psum[:, j, :], finished[(r, c)][:, j * P : (j + 1) * P], ident[:]
+                    )
+                first = e * FEATURES + c * P
+                target = out_rows[chunk][:, :, first : first + P]
+                if c % 2 == 0:
+                    nc.vector.tensor_copy(out=target, in_=o_psum[:])
+                else:
+                    nc.scalar.copy(out=target, in_=o_psum[:])
+            if e == EXPERTS - 1:
+                nc.sync.dma_start(
+                    out=out[chunk * CHUNK : (chunk + 1) * CHUNK, :].rearrange(
+                        "(p j) f -> p j f", j=ROW_BLOCKS
+                    ),
+                    in_=out_rows[chunk][:],
+                )
+
+        transpose_in(0)
+        quantise(0)
+        spread_vectors()
+        for r in range(ROUNDS + 1):
+            if r + 1 < ROUNDS:
+                transpose_in(r + 1)
+            if r >= 1:
+                transpose_out(r - 1)
+            if r + 1 < ROUNDS:
+                quantise(r + 1)
+            if r < ROUNDS:
+                multiply(r)

@@ -25,6 +25,7 @@ ROUNDS = CHUNKS * EXPERTS
 WORDS = K // 2
 VECTORS = 5
 COLUMNS = EXPERTS * FEATURE_BLOCKS
+OUT_LAG = 2
 
 FLOPS = 2 * ROWS * K * FEATURES * EXPERTS
 
@@ -38,11 +39,11 @@ def tile_mom_t_e_kernel(
     with tc.tile_pool(name="keep", bufs=1) as keep, tc.tile_pool(
         name="rows_in", bufs=1
     ) as rows_in, tc.tile_pool(name="quantised", bufs=2) as quantised, tc.tile_pool(
-        name="features_first", bufs=2 * FEATURE_BLOCKS
+        name="features_first", bufs=(OUT_LAG + 1) * FEATURE_BLOCKS
     ) as features_first, tc.tile_pool(name="rows_out", bufs=3) as rows_out, tc.psum_pool(
         name="psum_in", bufs=2
-    ) as psum_in, tc.psum_pool(name="psum_acc", bufs=3) as psum_acc, tc.psum_pool(
-        name="psum_out", bufs=3
+    ) as psum_in, tc.psum_pool(name="psum_acc", bufs=FEATURE_BLOCKS) as psum_acc, tc.psum_pool(
+        name="psum_out", bufs=2
     ) as psum_out, tc.manual_schedule():
         x_rows = []
         for r in range(ROUNDS):
@@ -113,24 +114,24 @@ def tile_mom_t_e_kernel(
         finished = {}
         out_rows = {}
 
-        def transpose_in(r):
+        def transpose_in(r, half):
+            if half == 0:
+                grouped[r] = quantised.tile([P, CHUNK * 4], BF16, name="grouped", align_bytes=64)
             words = x_rows[r][:].rearrange("p j k -> p (j k)").bitcast(F32)
-            grouped[r] = quantised.tile([P, CHUNK * 4], BF16, name="grouped", align_bytes=64)
             pairs = grouped[r][:].bitcast(F32).rearrange("p (n u) -> p n u", u=2)
-            for half in range(2):
-                x_psum = psum_in.tile([P, 2, CHUNK // 2], F32, tag="x_psum")
-                for jj in range(ROW_BLOCKS // 2):
-                    j = half * (ROW_BLOCKS // 2) + jj
-                    for u in range(2):
-                        nc.tensor.transpose(
-                            x_psum[:, u, jj * P : (jj + 1) * P],
-                            words[:, j * WORDS + u : (j + 1) * WORDS : 2],
-                            ident[:],
-                        )
-                nc.vector.tensor_copy(
-                    out=pairs[:, half * (CHUNK // 2) : (half + 1) * (CHUNK // 2), :],
-                    in_=x_psum[:].rearrange("p u n -> p n u"),
-                )
+            x_psum = psum_in.tile([P, 2, CHUNK // 2], F32, tag="x_psum")
+            for jj in range(ROW_BLOCKS // 2):
+                j = half * (ROW_BLOCKS // 2) + jj
+                for u in range(2):
+                    nc.tensor.transpose(
+                        x_psum[:, u, jj * P : (jj + 1) * P],
+                        words[:, j * WORDS + u : (j + 1) * WORDS : 2],
+                        ident[:],
+                    )
+            nc.vector.tensor_copy(
+                out=pairs[:, half * (CHUNK // 2) : (half + 1) * (CHUNK // 2), :],
+                in_=x_psum[:].rearrange("p u n -> p n u"),
+            )
 
         def quantise(r):
             x_codes[r] = quantised.tile([P, CHUNK], U32, name="x_codes", align_bytes=64)
@@ -158,7 +159,7 @@ def tile_mom_t_e_kernel(
                 nc.scalar.activation(
                     out=z[:], in_=acc[:], func=ACT.Gelu_apprx_sigmoid, bias=bias[:, col], scale=1.0
                 )
-                nc.vector.tensor_scalar(
+                nc.gpsimd.tensor_scalar(
                     out=z[:],
                     in0=z[:],
                     scalar1=gain[:, col],
@@ -168,25 +169,24 @@ def tile_mom_t_e_kernel(
                 )
                 finished[(r, c)] = z
 
-        def transpose_out(r):
+        def transpose_out(r, c):
             chunk, e = divmod(r, EXPERTS)
-            if e == 0:
+            if e == 0 and c == 0:
                 out_rows[chunk] = rows_out.tile(
                     [P, ROW_BLOCKS, EXPERTS * FEATURES], F32, name="out_rows"
                 )
-            for c in range(FEATURE_BLOCKS):
-                o_psum = psum_out.tile([P, ROW_BLOCKS, P], F32, name="o_psum")
-                for j in range(ROW_BLOCKS):
-                    nc.tensor.transpose(
-                        o_psum[:, j, :], finished[(r, c)][:, j * P : (j + 1) * P], ident[:]
-                    )
-                first = e * FEATURES + c * P
-                target = out_rows[chunk][:, :, first : first + P]
-                if c % 2 == 0:
-                    nc.vector.tensor_copy(out=target, in_=o_psum[:])
-                else:
-                    nc.scalar.copy(out=target, in_=o_psum[:])
-            if e == EXPERTS - 1:
+            o_psum = psum_out.tile([P, ROW_BLOCKS, P], F32, name="o_psum")
+            for j in range(ROW_BLOCKS):
+                nc.tensor.transpose(
+                    o_psum[:, j, :], finished[(r, c)][:, j * P : (j + 1) * P], ident[:]
+                )
+            first = e * FEATURES + c * P
+            target = out_rows[chunk][:, :, first : first + P]
+            if c == FEATURE_BLOCKS - 1:
+                nc.scalar.copy(out=target, in_=o_psum[:])
+            else:
+                nc.vector.tensor_copy(out=target, in_=o_psum[:])
+            if e == EXPERTS - 1 and c == FEATURE_BLOCKS - 1:
                 nc.sync.dma_start(
                     out=out[chunk * CHUNK : (chunk + 1) * CHUNK, :].rearrange(
                         "(p j) f -> p j f", j=ROW_BLOCKS
@@ -194,14 +194,17 @@ def tile_mom_t_e_kernel(
                     in_=out_rows[chunk][:],
                 )
 
-        transpose_in(0)
+        transpose_in(0, 0)
+        transpose_in(0, 1)
         quantise(0)
         spread_vectors()
-        for r in range(ROUNDS + 1):
-            if r + 1 < ROUNDS:
-                transpose_in(r + 1)
-            if r >= 1:
-                transpose_out(r - 1)
+        for r in range(ROUNDS + OUT_LAG):
+            for half in range(2):
+                if r >= OUT_LAG:
+                    transpose_out(r - OUT_LAG, 2 * half)
+                    transpose_out(r - OUT_LAG, 2 * half + 1)
+                if r + 1 < ROUNDS:
+                    transpose_in(r + 1, half)
             if r + 1 < ROUNDS:
                 quantise(r + 1)
             if r < ROUNDS:

@@ -26,6 +26,7 @@ WORDS = K // 2
 VECTORS = 5
 COLUMNS = EXPERTS * FEATURE_BLOCKS
 OUT_LAG = 2
+IN_LEAD = 2
 
 FLOPS = 2 * ROWS * K * FEATURES * EXPERTS
 
@@ -38,7 +39,7 @@ def tile_mom_t_e_kernel(
 
     with tc.tile_pool(name="keep", bufs=1) as keep, tc.tile_pool(
         name="rows_in", bufs=1
-    ) as rows_in, tc.tile_pool(name="quantised", bufs=2) as quantised, tc.tile_pool(
+    ) as rows_in, tc.tile_pool(name="quantised", bufs=IN_LEAD + 1) as quantised, tc.tile_pool(
         name="features_first", bufs=(OUT_LAG + 1) * FEATURE_BLOCKS
     ) as features_first, tc.tile_pool(name="rows_out", bufs=3) as rows_out, tc.psum_pool(
         name="psum_in", bufs=2
@@ -140,34 +141,33 @@ def tile_mom_t_e_kernel(
                 out=x_codes[r][:].bitcast(FP8X4), scales=x_scales[r][:], in_=grouped[r][:]
             )
 
-        def multiply(r):
+        def multiply(r, c):
             e = r % EXPERTS
-            for c in range(FEATURE_BLOCKS):
-                cols = slice(c * P, (c + 1) * P)
-                col = slice(e * FEATURE_BLOCKS + c, e * FEATURE_BLOCKS + c + 1)
-                acc = psum_acc.tile([P, CHUNK], F32, name="acc")
-                nc.tensor.matmul_mx(
-                    out=acc[:],
-                    lhsT=w_codes[:, e, cols].bitcast(FP8X4),
-                    lhsT_scale=w_scales[:, e, cols],
-                    rhs=x_codes[r][:].bitcast(FP8X4),
-                    rhs_scale=x_scales[r][:],
-                    start=True,
-                    stop=True,
-                )
-                z = features_first.tile([P, CHUNK], F32, name="z")
-                nc.scalar.activation(
-                    out=z[:], in_=acc[:], func=ACT.Gelu_apprx_sigmoid, bias=bias[:, col], scale=1.0
-                )
-                nc.gpsimd.tensor_scalar(
-                    out=z[:],
-                    in0=z[:],
-                    scalar1=gain[:, col],
-                    scalar2=shift[:, col],
-                    op0=ALU.mult,
-                    op1=ALU.add,
-                )
-                finished[(r, c)] = z
+            cols = slice(c * P, (c + 1) * P)
+            col = slice(e * FEATURE_BLOCKS + c, e * FEATURE_BLOCKS + c + 1)
+            acc = psum_acc.tile([P, CHUNK], F32, name="acc")
+            nc.tensor.matmul_mx(
+                out=acc[:],
+                lhsT=w_codes[:, e, cols].bitcast(FP8X4),
+                lhsT_scale=w_scales[:, e, cols],
+                rhs=x_codes[r][:].bitcast(FP8X4),
+                rhs_scale=x_scales[r][:],
+                start=True,
+                stop=True,
+            )
+            z = features_first.tile([P, CHUNK], F32, name="z")
+            nc.scalar.activation(
+                out=z[:], in_=acc[:], func=ACT.Gelu_apprx_sigmoid, bias=bias[:, col], scale=1.0
+            )
+            nc.gpsimd.tensor_scalar(
+                out=z[:],
+                in0=z[:],
+                scalar1=gain[:, col],
+                scalar2=shift[:, col],
+                op0=ALU.mult,
+                op1=ALU.add,
+            )
+            finished[(r, c)] = z
 
         def transpose_out(r, c):
             chunk, e = divmod(r, EXPERTS)
@@ -194,18 +194,21 @@ def tile_mom_t_e_kernel(
                     in_=out_rows[chunk][:],
                 )
 
-        transpose_in(0, 0)
-        transpose_in(0, 1)
-        quantise(0)
+        for r in range(IN_LEAD):
+            transpose_in(r, 0)
+            transpose_in(r, 1)
+            if r == 0:
+                quantise(0)
         spread_vectors()
         for r in range(ROUNDS + OUT_LAG):
+            if r + 1 < ROUNDS:
+                quantise(r + 1)
             for half in range(2):
                 if r >= OUT_LAG:
                     transpose_out(r - OUT_LAG, 2 * half)
                     transpose_out(r - OUT_LAG, 2 * half + 1)
-                if r + 1 < ROUNDS:
-                    transpose_in(r + 1, half)
-            if r + 1 < ROUNDS:
-                quantise(r + 1)
-            if r < ROUNDS:
-                multiply(r)
+                if r + IN_LEAD < ROUNDS:
+                    transpose_in(r + IN_LEAD, half)
+                if r < ROUNDS:
+                    multiply(r, 2 * half)
+                    multiply(r, 2 * half + 1)

@@ -41,10 +41,10 @@ def tile_mom_t_e_kernel(
         name="rows_in", bufs=1
     ) as rows_in, tc.tile_pool(name="quantised", bufs=IN_LEAD + 1) as quantised, tc.tile_pool(
         name="features_first", bufs=(OUT_LAG + 1) * FEATURE_BLOCKS
-    ) as features_first, tc.tile_pool(name="rows_out", bufs=3) as rows_out, tc.psum_pool(
+    ) as features_first, tc.tile_pool(name="rows_out", bufs=4) as rows_out, tc.psum_pool(
         name="psum_in", bufs=2
-    ) as psum_in, tc.psum_pool(name="psum_acc", bufs=FEATURE_BLOCKS) as psum_acc, tc.psum_pool(
-        name="psum_out", bufs=2
+    ) as psum_in, tc.psum_pool(name="psum_acc", bufs=3) as psum_acc, tc.psum_pool(
+        name="psum_out", bufs=3
     ) as psum_out, tc.manual_schedule():
         x_rows = []
         for r in range(ROUNDS):
@@ -159,7 +159,13 @@ def tile_mom_t_e_kernel(
             nc.scalar.activation(
                 out=z[:], in_=acc[:], func=ACT.Gelu_apprx_sigmoid, bias=bias[:, col], scale=1.0
             )
-            nc.gpsimd.tensor_scalar(
+            finished[(r, c)] = z
+
+        def normalise(r, c):
+            col = slice((r % EXPERTS) * FEATURE_BLOCKS + c, (r % EXPERTS) * FEATURE_BLOCKS + c + 1)
+            z = finished[(r, c)]
+            engine = nc.gpsimd if c % 2 == 0 else nc.vector
+            engine.tensor_scalar(
                 out=z[:],
                 in0=z[:],
                 scalar1=gain[:, col],
@@ -167,31 +173,27 @@ def tile_mom_t_e_kernel(
                 op0=ALU.mult,
                 op1=ALU.add,
             )
-            finished[(r, c)] = z
 
         def transpose_out(r, c):
             chunk, e = divmod(r, EXPERTS)
-            if e == 0 and c == 0:
-                out_rows[chunk] = rows_out.tile(
-                    [P, ROW_BLOCKS, EXPERTS * FEATURES], F32, name="out_rows"
-                )
+            if c == 0:
+                out_rows[r] = rows_out.tile([P, ROW_BLOCKS, FEATURES], F32, name="out_rows")
             o_psum = psum_out.tile([P, ROW_BLOCKS, P], F32, name="o_psum")
             for j in range(ROW_BLOCKS):
                 nc.tensor.transpose(
                     o_psum[:, j, :], finished[(r, c)][:, j * P : (j + 1) * P], ident[:]
                 )
-            first = e * FEATURES + c * P
-            target = out_rows[chunk][:, :, first : first + P]
-            if c == FEATURE_BLOCKS - 1:
-                nc.scalar.copy(out=target, in_=o_psum[:])
-            else:
+            target = out_rows[r][:, :, c * P : (c + 1) * P]
+            if c % 2 == 0:
                 nc.vector.tensor_copy(out=target, in_=o_psum[:])
-            if e == EXPERTS - 1 and c == FEATURE_BLOCKS - 1:
+            else:
+                nc.scalar.copy(out=target, in_=o_psum[:])
+            if c == FEATURE_BLOCKS - 1:
                 nc.sync.dma_start(
-                    out=out[chunk * CHUNK : (chunk + 1) * CHUNK, :].rearrange(
-                        "(p j) f -> p j f", j=ROW_BLOCKS
-                    ),
-                    in_=out_rows[chunk][:],
+                    out=out[
+                        chunk * CHUNK : (chunk + 1) * CHUNK, e * FEATURES : (e + 1) * FEATURES
+                    ].rearrange("(p j) f -> p j f", j=ROW_BLOCKS),
+                    in_=out_rows[r][:],
                 )
 
         for r in range(IN_LEAD):
@@ -200,15 +202,19 @@ def tile_mom_t_e_kernel(
             if r == 0:
                 quantise(0)
         spread_vectors()
-        for r in range(ROUNDS + OUT_LAG):
-            if r + 1 < ROUNDS:
+        for step in range(2 * (ROUNDS + OUT_LAG)):
+            r, half = divmod(step, 2)
+            if half == 0 and r + 1 < ROUNDS:
                 quantise(r + 1)
-            for half in range(2):
-                if r >= OUT_LAG:
-                    transpose_out(r - OUT_LAG, 2 * half)
-                    transpose_out(r - OUT_LAG, 2 * half + 1)
-                if r + IN_LEAD < ROUNDS:
-                    transpose_in(r + IN_LEAD, half)
-                if r < ROUNDS:
-                    multiply(r, 2 * half)
-                    multiply(r, 2 * half + 1)
+            if r >= OUT_LAG:
+                transpose_out(r - OUT_LAG, 2 * half)
+                transpose_out(r - OUT_LAG, 2 * half + 1)
+            if r + IN_LEAD < ROUNDS:
+                transpose_in(r + IN_LEAD, half)
+            if 1 <= step <= 2 * ROUNDS:
+                last_r, last_half = divmod(step - 1, 2)
+                normalise(last_r, 2 * last_half)
+                normalise(last_r, 2 * last_half + 1)
+            if r < ROUNDS:
+                multiply(r, 2 * half)
+                multiply(r, 2 * half + 1)

@@ -27,6 +27,7 @@ VECTORS = 5
 COLUMNS = EXPERTS * FEATURE_BLOCKS
 OUT_LAG = 2
 IN_LEAD = 2
+OUT_BUFS = 8
 
 FLOPS = 2 * ROWS * K * FEATURES * EXPERTS
 
@@ -41,7 +42,7 @@ def tile_mom_t_e_kernel(
         name="rows_in", bufs=1
     ) as rows_in, tc.tile_pool(name="quantised", bufs=IN_LEAD + 1) as quantised, tc.tile_pool(
         name="features_first", bufs=(OUT_LAG + 1) * FEATURE_BLOCKS
-    ) as features_first, tc.tile_pool(name="rows_out", bufs=4) as rows_out, tc.psum_pool(
+    ) as features_first, tc.tile_pool(name="rows_out", bufs=OUT_BUFS) as rows_out, tc.psum_pool(
         name="psum_in", bufs=2
     ) as psum_in, tc.psum_pool(name="psum_acc", bufs=3) as psum_acc, tc.psum_pool(
         name="psum_out", bufs=3
@@ -59,9 +60,20 @@ def tile_mom_t_e_kernel(
                 ),
             )
 
+        vec_rows = keep.tile([P, P], BF16)
+        nc.vector.memset(vec_rows[:], 0.0)
+        for v, vec in enumerate([b, gamma, beta, running_mean, running_var]):
+            nc.scalar.dma_start(
+                out=vec_rows[v * COLUMNS : (v + 1) * COLUMNS, :],
+                in_=vec.rearrange("o e (c f) -> (o e c) f", f=P),
+            )
+        ident = keep.tile([P, P], F32)
+        make_identity(nc, ident[:])
+
+        for r in range(IN_LEAD + 1):
+            load_rows(r)
         w_scales = keep.tile([P, EXPERTS, FEATURES], U8, align_bytes=64)
         nc.vector.memset(w_scales[:].rearrange("p g n -> p (g n)").bitcast(I32), 0)
-        load_rows(0)
         for quadrant in range(4):
             nc.sync.dma_start(
                 out=w_scales[32 * quadrant : 32 * quadrant + 4, :, :].bitcast(I32),
@@ -75,19 +87,10 @@ def tile_mom_t_e_kernel(
                 out=w_codes[:, e, :].bitcast(I32),
                 in_=W_words[e].rearrange("p n t -> p (n t)").bitcast(I32),
             )
-            load_rows(e + 1)
-        for r in range(EXPERTS + 1, ROUNDS):
+            load_rows(IN_LEAD + 1 + e)
+        for r in range(IN_LEAD + 1 + EXPERTS, ROUNDS):
             load_rows(r)
 
-        ident = keep.tile([P, P], F32)
-        make_identity(nc, ident[:])
-        vec_rows = keep.tile([P, P], BF16)
-        nc.vector.memset(vec_rows[:], 0.0)
-        for v, vec in enumerate([b, gamma, beta, running_mean, running_var]):
-            nc.scalar.dma_start(
-                out=vec_rows[v * COLUMNS : (v + 1) * COLUMNS, :],
-                in_=vec.rearrange("o e (c f) -> (o e c) f", f=P),
-            )
         vec_cols = keep.tile([P, VECTORS, COLUMNS], F32)
         bias = vec_cols[:, 0, :]
         gain = keep.tile([P, COLUMNS], F32)
@@ -196,12 +199,12 @@ def tile_mom_t_e_kernel(
                     in_=out_rows[r][:],
                 )
 
+        spread_vectors()
         for r in range(IN_LEAD):
             transpose_in(r, 0)
             transpose_in(r, 1)
             if r == 0:
                 quantise(0)
-        spread_vectors()
         for step in range(2 * (ROUNDS + OUT_LAG)):
             r, half = divmod(step, 2)
             if half == 0 and r + 1 < ROUNDS:

@@ -25,7 +25,7 @@ ROUNDS = CHUNKS * EXPERTS
 WORDS = K // 2
 VECTORS = 5
 COLUMNS = EXPERTS * FEATURE_BLOCKS
-OUT_LAG = 2
+OUT_LAG = 1
 IN_LEAD = 2
 OUT_BUFS = 8
 
@@ -42,11 +42,7 @@ def tile_mom_t_e_kernel(
         name="rows_in", bufs=1
     ) as rows_in, tc.tile_pool(name="quantised", bufs=IN_LEAD + 1) as quantised, tc.tile_pool(
         name="features_first", bufs=(OUT_LAG + 1) * FEATURE_BLOCKS
-    ) as features_first, tc.tile_pool(name="rows_out", bufs=OUT_BUFS) as rows_out, tc.psum_pool(
-        name="psum_in", bufs=2
-    ) as psum_in, tc.psum_pool(name="psum_acc", bufs=3) as psum_acc, tc.psum_pool(
-        name="psum_out", bufs=3
-    ) as psum_out, tc.manual_schedule():
+    ) as features_first, tc.tile_pool(name="rows_out", bufs=OUT_BUFS) as rows_out, tc.psum_pool(name="psum", bufs=8) as psum, tc.manual_schedule():
         x_rows = []
         for r in range(ROUNDS):
             x_rows.append(rows_in.tile([P, ROW_BLOCKS, K], BF16, name="x_rows%d" % r))
@@ -99,7 +95,7 @@ def tile_mom_t_e_kernel(
         def spread_vectors():
             vec_rows_f32 = keep.tile([P, P], F32)
             nc.vector.tensor_copy(out=vec_rows_f32[:], in_=vec_rows[:])
-            vec_psum = psum_in.tile([P, P], F32, tag="x_psum")
+            vec_psum = psum.tile([P, P], F32, tag="bank")
             nc.tensor.transpose(vec_psum[:], vec_rows_f32[:], ident[:])
             nc.vector.tensor_copy(
                 out=vec_cols[:].rearrange("p v c -> p (v c)"),
@@ -123,7 +119,7 @@ def tile_mom_t_e_kernel(
                 grouped[r] = quantised.tile([P, CHUNK * 4], BF16, name="grouped", align_bytes=64)
             words = x_rows[r][:].rearrange("p j k -> p (j k)").bitcast(F32)
             pairs = grouped[r][:].bitcast(F32).rearrange("p (n u) -> p n u", u=2)
-            x_psum = psum_in.tile([P, 2, CHUNK // 2], F32, tag="x_psum")
+            x_psum = psum.tile([P, 2, CHUNK // 2], F32, tag="bank")
             for jj in range(ROW_BLOCKS // 2):
                 j = half * (ROW_BLOCKS // 2) + jj
                 for u in range(2):
@@ -148,7 +144,7 @@ def tile_mom_t_e_kernel(
             e = r % EXPERTS
             cols = slice(c * P, (c + 1) * P)
             col = slice(e * FEATURE_BLOCKS + c, e * FEATURE_BLOCKS + c + 1)
-            acc = psum_acc.tile([P, CHUNK], F32, name="acc")
+            acc = psum.tile([P, CHUNK], F32, tag="bank")
             nc.tensor.matmul_mx(
                 out=acc[:],
                 lhsT=w_codes[:, e, cols].bitcast(FP8X4),
@@ -181,7 +177,7 @@ def tile_mom_t_e_kernel(
             chunk, e = divmod(r, EXPERTS)
             if c == 0:
                 out_rows[r] = rows_out.tile([P, ROW_BLOCKS, FEATURES], F32, name="out_rows")
-            o_psum = psum_out.tile([P, ROW_BLOCKS, P], F32, name="o_psum")
+            o_psum = psum.tile([P, ROW_BLOCKS, P], F32, tag="bank")
             for j in range(ROW_BLOCKS):
                 nc.tensor.transpose(
                     o_psum[:, j, :], finished[(r, c)][:, j * P : (j + 1) * P], ident[:]
@@ -205,19 +201,20 @@ def tile_mom_t_e_kernel(
             transpose_in(r, 1)
             if r == 0:
                 quantise(0)
-        for step in range(2 * (ROUNDS + OUT_LAG)):
-            r, half = divmod(step, 2)
-            if half == 0 and r + 1 < ROUNDS:
+        for r in range(ROUNDS + OUT_LAG):
+            if r + 1 < ROUNDS:
                 quantise(r + 1)
-            if r >= OUT_LAG:
-                transpose_out(r - OUT_LAG, 2 * half)
-                transpose_out(r - OUT_LAG, 2 * half + 1)
-            if r + IN_LEAD < ROUNDS:
-                transpose_in(r + IN_LEAD, half)
-            if 1 <= step <= 2 * ROUNDS:
-                last_r, last_half = divmod(step - 1, 2)
-                normalise(last_r, 2 * last_half)
-                normalise(last_r, 2 * last_half + 1)
             if r < ROUNDS:
-                multiply(r, 2 * half)
-                multiply(r, 2 * half + 1)
+                for c in range(FEATURE_BLOCKS):
+                    multiply(r, c)
+                    if c % 2 == 0:
+                        normalise(r, c)
+            if r + IN_LEAD < ROUNDS:
+                transpose_in(r + IN_LEAD, 0)
+                transpose_in(r + IN_LEAD, 1)
+            if r < ROUNDS:
+                normalise(r, 1)
+                normalise(r, 3)
+            if r >= OUT_LAG:
+                for c in range(FEATURE_BLOCKS):
+                    transpose_out(r - OUT_LAG, c)

@@ -163,8 +163,7 @@ def tile_mom_t_e_kernel(
         def normalise(r, c):
             col = slice((r % EXPERTS) * FEATURE_BLOCKS + c, (r % EXPERTS) * FEATURE_BLOCKS + c + 1)
             z = finished[(r, c)]
-            engine = nc.gpsimd if c % 2 == 0 else nc.vector
-            engine.tensor_scalar(
+            nc.gpsimd.tensor_scalar(
                 out=z[:],
                 in0=z[:],
                 scalar1=gain[:, col],
@@ -183,7 +182,7 @@ def tile_mom_t_e_kernel(
                     o_psum[:, j, :], finished[(r, c)][:, j * P : (j + 1) * P], ident[:]
                 )
             target = out_rows[r][:, :, c * P : (c + 1) * P]
-            if c % 2 == 0:
+            if c % 2 == 0 or (c == 3 and r % 2 == 0):
                 nc.vector.tensor_copy(out=target, in_=o_psum[:])
             else:
                 nc.scalar.copy(out=target, in_=o_psum[:])
@@ -207,14 +206,10 @@ def tile_mom_t_e_kernel(
             if r < ROUNDS:
                 for c in range(FEATURE_BLOCKS):
                     multiply(r, c)
-                    if c % 2 == 0:
-                        normalise(r, c)
+                    normalise(r, c)
             if r + IN_LEAD < ROUNDS:
                 transpose_in(r + IN_LEAD, 0)
                 transpose_in(r + IN_LEAD, 1)
-            if r < ROUNDS:
-                normalise(r, 1)
-                normalise(r, 3)
             if r >= OUT_LAG:
                 for c in range(FEATURE_BLOCKS):
                     transpose_out(r - OUT_LAG, c)

@@ -47,27 +47,30 @@ def tile_mom_t_e_kernel(
         for r in range(ROUNDS):
             x_rows.append(rows_in.tile([P, ROW_BLOCKS, K], BF16, name="x_rows%d" % r))
 
-        def load_rows(r):
+        def load_rows(r, pieces=1):
             chunk, e = divmod(r, EXPERTS)
-            nc.sync.dma_start(
-                out=x_rows[r][:],
-                in_=xs[e][chunk * CHUNK : (chunk + 1) * CHUNK, :].rearrange(
-                    "(p j) k -> p j k", j=ROW_BLOCKS
-                ),
+            rows = xs[e][chunk * CHUNK : (chunk + 1) * CHUNK, :].rearrange(
+                "(p j) k -> p j k", j=ROW_BLOCKS
             )
+            step = ROW_BLOCKS // pieces
+            for j in range(0, ROW_BLOCKS, step):
+                nc.sync.dma_start(out=x_rows[r][:, j : j + step, :], in_=rows[:, j : j + step, :])
 
         vec_rows = keep.tile([P, P], BF16)
         nc.vector.memset(vec_rows[:], 0.0)
         for v, vec in enumerate([b, gamma, beta, running_mean, running_var]):
-            nc.scalar.dma_start(
+            nc.sync.dma_start(
                 out=vec_rows[v * COLUMNS : (v + 1) * COLUMNS, :],
                 in_=vec.rearrange("o e (c f) -> (o e c) f", f=P),
             )
         ident = keep.tile([P, P], F32)
         make_identity(nc, ident[:])
+        warm = keep.tile([P, 2], F32)
+        nc.vector.memset(warm[:], 1.0)
+        nc.scalar.sqrt(out=warm[:, 1:2], in_=warm[:, 0:1])
 
-        for r in range(IN_LEAD + 1):
-            load_rows(r)
+        load_rows(0, pieces=2)
+        load_rows(1)
         w_scales = keep.tile([P, EXPERTS, FEATURES], U8, align_bytes=64)
         nc.vector.memset(w_scales[:].rearrange("p g n -> p (g n)").bitcast(I32), 0)
         for quadrant in range(4):
@@ -83,8 +86,8 @@ def tile_mom_t_e_kernel(
                 out=w_codes[:, e, :].bitcast(I32),
                 in_=W_words[e].rearrange("p n t -> p (n t)").bitcast(I32),
             )
-            load_rows(IN_LEAD + 1 + e)
-        for r in range(IN_LEAD + 1 + EXPERTS, ROUNDS):
+            load_rows(IN_LEAD + e)
+        for r in range(IN_LEAD + EXPERTS, ROUNDS):
             load_rows(r)
 
         vec_cols = keep.tile([P, VECTORS, COLUMNS], F32)
@@ -103,6 +106,7 @@ def tile_mom_t_e_kernel(
             )
             nc.vector.tensor_scalar_add(out=gain[:], in0=vec_cols[:, 4, :], scalar1=EPS)
             nc.scalar.sqrt(out=gain[:], in_=gain[:])
+            nc.scalar.activation(out=warm[:, 1:2], in_=warm[:, 0:1], func=ACT.Gelu_apprx_sigmoid)
             nc.vector.reciprocal(out=gain[:], in_=gain[:])
             nc.vector.tensor_mul(out=gain[:], in0=gain[:], in1=vec_cols[:, 1, :])
             nc.vector.tensor_mul(out=shift[:], in0=gain[:], in1=vec_cols[:, 3, :])

@@ -167,14 +167,19 @@ def tile_mom_t_e_kernel(
         def normalise(r, c):
             col = slice((r % EXPERTS) * FEATURE_BLOCKS + c, (r % EXPERTS) * FEATURE_BLOCKS + c + 1)
             z = finished[(r, c)]
-            nc.gpsimd.tensor_scalar(
-                out=z[:],
-                in0=z[:],
-                scalar1=gain[:, col],
-                scalar2=shift[:, col],
-                op0=ALU.mult,
-                op1=ALU.add,
-            )
+            if c < FEATURE_BLOCKS - 1:
+                nc.gpsimd.tensor_scalar(
+                    out=z[:],
+                    in0=z[:],
+                    scalar1=gain[:, col],
+                    scalar2=shift[:, col],
+                    op0=ALU.mult,
+                    op1=ALU.add,
+                )
+            else:
+                nc.scalar.activation(
+                    out=z[:], in_=z[:], func=ACT.Identity, bias=shift[:, col], scale=gain[:, col]
+                )
 
         def transpose_out(r, c):
             chunk, e = divmod(r, EXPERTS)
@@ -186,7 +191,7 @@ def tile_mom_t_e_kernel(
                     o_psum[:, j, :], finished[(r, c)][:, j * P : (j + 1) * P], ident[:]
                 )
             target = out_rows[r][:, :, c * P : (c + 1) * P]
-            if c % 2 == 0 or (c == 3 and r % 2 == 0):
+            if c != 1:
                 nc.vector.tensor_copy(out=target, in_=o_psum[:])
             else:
                 nc.scalar.copy(out=target, in_=o_psum[:])

@@ -47,14 +47,14 @@ def tile_mom_t_e_kernel(
         for r in range(ROUNDS):
             x_rows.append(rows_in.tile([P, ROW_BLOCKS, K], BF16, name="x_rows%d" % r))
 
-        def load_rows(r, pieces=1):
+        def load_rows(r):
             chunk, e = divmod(r, EXPERTS)
-            rows = xs[e][chunk * CHUNK : (chunk + 1) * CHUNK, :].rearrange(
-                "(p j) k -> p j k", j=ROW_BLOCKS
+            nc.sync.dma_start(
+                out=x_rows[r][:],
+                in_=xs[e][chunk * CHUNK : (chunk + 1) * CHUNK, :].rearrange(
+                    "(p j) k -> p j k", j=ROW_BLOCKS
+                ),
             )
-            step = ROW_BLOCKS // pieces
-            for j in range(0, ROW_BLOCKS, step):
-                nc.sync.dma_start(out=x_rows[r][:, j : j + step, :], in_=rows[:, j : j + step, :])
 
         vec_rows = keep.tile([P, P], BF16)
         nc.vector.memset(vec_rows[:], 0.0)
@@ -69,7 +69,7 @@ def tile_mom_t_e_kernel(
         nc.vector.memset(warm[:], 1.0)
         nc.scalar.sqrt(out=warm[:, 1:2], in_=warm[:, 0:1])
 
-        load_rows(0, pieces=2)
+        load_rows(0)
         load_rows(1)
         w_scales = keep.tile([P, EXPERTS, FEATURES], U8, align_bytes=64)
         nc.vector.memset(w_scales[:].rearrange("p g n -> p (g n)").bitcast(I32), 0)
@@ -191,7 +191,13 @@ def tile_mom_t_e_kernel(
                     o_psum[:, j, :], finished[(r, c)][:, j * P : (j + 1) * P], ident[:]
                 )
             target = out_rows[r][:, :, c * P : (c + 1) * P]
-            if c != 1:
+            if r == ROUNDS - 1:
+                on_vector = c % 2 == 0
+            elif r + OUT_LAG + IN_LEAD >= ROUNDS:
+                on_vector = True
+            else:
+                on_vector = c != 1
+            if on_vector:
                 nc.vector.tensor_copy(out=target, in_=o_psum[:])
             else:
                 nc.scalar.copy(out=target, in_=o_psum[:])

@@ -27,7 +27,8 @@ VECTORS = 5
 COLUMNS = EXPERTS * FEATURE_BLOCKS
 OUT_LAG = 1
 IN_LEAD = 2
-OUT_BUFS = 8
+OUT_BUFS = 3
+AHEAD = 12
 
 FLOPS = 2 * ROWS * K * FEATURES * EXPERTS
 
@@ -87,7 +88,7 @@ def tile_mom_t_e_kernel(
                 in_=W_words[e].rearrange("p n t -> p (n t)").bitcast(I32),
             )
             load_rows(IN_LEAD + e)
-        for r in range(IN_LEAD + EXPERTS, ROUNDS):
+        for r in range(IN_LEAD + EXPERTS, AHEAD):
             load_rows(r)
 
         vec_cols = keep.tile([P, VECTORS, COLUMNS], F32)
@@ -183,14 +184,16 @@ def tile_mom_t_e_kernel(
 
         def transpose_out(r, c):
             chunk, e = divmod(r, EXPERTS)
-            if c == 0:
-                out_rows[r] = rows_out.tile([P, ROW_BLOCKS, FEATURES], F32, name="out_rows")
+            if c == 0 and e == 0:
+                out_rows[chunk] = rows_out.tile(
+                    [P, ROW_BLOCKS, EXPERTS * FEATURES], F32, name="out_rows"
+                )
             o_psum = psum.tile([P, ROW_BLOCKS, P], F32, tag="bank")
             for j in range(ROW_BLOCKS):
                 nc.tensor.transpose(
                     o_psum[:, j, :], finished[(r, c)][:, j * P : (j + 1) * P], ident[:]
                 )
-            target = out_rows[r][:, :, c * P : (c + 1) * P]
+            target = out_rows[chunk][:, :, e * FEATURES + c * P : e * FEATURES + (c + 1) * P]
             if r == ROUNDS - 1:
                 on_vector = c % 2 == 0
             elif r + OUT_LAG + IN_LEAD >= ROUNDS:
@@ -202,12 +205,17 @@ def tile_mom_t_e_kernel(
             else:
                 nc.scalar.copy(out=target, in_=o_psum[:])
             if c == FEATURE_BLOCKS - 1:
-                nc.sync.dma_start(
-                    out=out[
-                        chunk * CHUNK : (chunk + 1) * CHUNK, e * FEATURES : (e + 1) * FEATURES
-                    ].rearrange("(p j) f -> p j f", j=ROW_BLOCKS),
-                    in_=out_rows[r][:],
+                rows = out[chunk * CHUNK : (chunk + 1) * CHUNK, :].rearrange(
+                    "(p j) f -> p j f", j=ROW_BLOCKS
                 )
+                if chunk >= CHUNKS - 2:
+                    cols = slice(e * FEATURES, (e + 1) * FEATURES)
+                    nc.sync.dma_start(out=rows[:, :, cols], in_=out_rows[chunk][:, :, cols])
+                elif e == EXPERTS - 1:
+                    nc.sync.dma_start(out=rows, in_=out_rows[chunk][:])
+                    for later in range(r + 1 + AHEAD - EXPERTS, r + 1 + AHEAD):
+                        if later < ROUNDS:
+                            load_rows(later)
 
         spread_vectors()
         for r in range(IN_LEAD):

@@ -23,7 +23,6 @@ FEATURE_BLOCKS = FEATURES // P
 CHUNKS = ROWS // CHUNK
 ROUNDS = CHUNKS * EXPERTS
 WORDS = K // 2
-VECTORS = 5
 COLUMNS = EXPERTS * FEATURE_BLOCKS
 OUT_LAG = 1
 IN_LEAD = 2
@@ -57,21 +56,28 @@ def tile_mom_t_e_kernel(
                 ),
             )
 
-        vec_rows = keep.tile([P, P], BF16)
-        nc.vector.memset(vec_rows[:], 0.0)
-        for v, vec in enumerate([b, gamma, beta, running_mean, running_var]):
-            nc.sync.dma_start(
-                out=vec_rows[v * COLUMNS : (v + 1) * COLUMNS, :],
-                in_=vec.rearrange("o e (c f) -> (o e c) f", f=P),
-            )
+        load_rows(0)
+        load_rows(1)
+
+        first_rows = keep.tile([P, P], BF16)
+        nc.vector.memset(first_rows[:], 0.0)
+        second_rows = keep.tile([P, P], BF16)
+        nc.vector.memset(second_rows[:], 0.0)
         ident = keep.tile([P, P], F32)
         make_identity(nc, ident[:])
+        for rows_tile, vectors in (
+            (first_rows, [running_var, b]),
+            (second_rows, [gamma, beta, running_mean]),
+        ):
+            for v, vec in enumerate(vectors):
+                nc.gpsimd.dma_start(
+                    out=rows_tile[v * COLUMNS : (v + 1) * COLUMNS, :],
+                    in_=vec.rearrange("o e (c f) -> (o e c) f", f=P),
+                )
         warm = keep.tile([P, 2], F32)
         nc.vector.memset(warm[:], 1.0)
         nc.scalar.sqrt(out=warm[:, 1:2], in_=warm[:, 0:1])
 
-        load_rows(0)
-        load_rows(1)
         w_scales = keep.tile([P, EXPERTS, FEATURES], U8, align_bytes=64)
         nc.vector.memset(w_scales[:].rearrange("p g n -> p (g n)").bitcast(I32), 0)
         for quadrant in range(4):
@@ -91,27 +97,36 @@ def tile_mom_t_e_kernel(
         for r in range(IN_LEAD + EXPERTS, AHEAD):
             load_rows(r)
 
-        vec_cols = keep.tile([P, VECTORS, COLUMNS], F32)
-        bias = vec_cols[:, 0, :]
+        first_cols = keep.tile([P, 2, COLUMNS], F32)
+        bias = first_cols[:, 1, :]
+        second_cols = keep.tile([P, 3, COLUMNS], F32)
         gain = keep.tile([P, COLUMNS], F32)
         shift = keep.tile([P, COLUMNS], F32)
 
-        def spread_vectors():
-            vec_rows_f32 = keep.tile([P, P], F32)
-            nc.vector.tensor_copy(out=vec_rows_f32[:], in_=vec_rows[:])
-            vec_psum = psum.tile([P, P], F32, tag="bank")
-            nc.tensor.transpose(vec_psum[:], vec_rows_f32[:], ident[:])
-            nc.vector.tensor_copy(
-                out=vec_cols[:].rearrange("p v c -> p (v c)"),
-                in_=vec_psum[:, : VECTORS * COLUMNS],
+        def spread_first():
+            first_f32 = keep.tile([P, P], F32)
+            nc.scalar.copy(out=first_f32[:], in_=first_rows[:])
+            first_psum = psum.tile([P, P], F32, tag="bank")
+            nc.tensor.transpose(first_psum[:], first_f32[:], ident[:])
+            nc.scalar.copy(
+                out=first_cols[:].rearrange("p v c -> p (v c)"), in_=first_psum[:, : 2 * COLUMNS]
             )
-            nc.vector.tensor_scalar_add(out=gain[:], in0=vec_cols[:, 4, :], scalar1=EPS)
+            nc.vector.tensor_scalar_add(out=gain[:], in0=first_cols[:, 0, :], scalar1=EPS)
             nc.scalar.sqrt(out=gain[:], in_=gain[:])
             nc.scalar.activation(out=warm[:, 1:2], in_=warm[:, 0:1], func=ACT.Gelu_apprx_sigmoid)
+
+        def spread_second():
+            second_f32 = keep.tile([P, P], F32)
+            nc.vector.tensor_copy(out=second_f32[:], in_=second_rows[:])
+            second_psum = psum.tile([P, P], F32, tag="bank")
+            nc.tensor.transpose(second_psum[:], second_f32[:], ident[:])
+            nc.vector.tensor_copy(
+                out=second_cols[:].rearrange("p v c -> p (v c)"), in_=second_psum[:, : 3 * COLUMNS]
+            )
             nc.vector.reciprocal(out=gain[:], in_=gain[:])
-            nc.vector.tensor_mul(out=gain[:], in0=gain[:], in1=vec_cols[:, 1, :])
-            nc.vector.tensor_mul(out=shift[:], in0=gain[:], in1=vec_cols[:, 3, :])
-            nc.vector.tensor_sub(out=shift[:], in0=vec_cols[:, 2, :], in1=shift[:])
+            nc.vector.tensor_mul(out=gain[:], in0=gain[:], in1=second_cols[:, 0, :])
+            nc.vector.tensor_mul(out=shift[:], in0=gain[:], in1=second_cols[:, 2, :])
+            nc.vector.tensor_sub(out=shift[:], in0=second_cols[:, 1, :], in1=shift[:])
 
         grouped = {}
         x_codes = {}
@@ -217,18 +232,21 @@ def tile_mom_t_e_kernel(
                         if later < ROUNDS:
                             load_rows(later)
 
-        spread_vectors()
-        for r in range(IN_LEAD):
-            transpose_in(r, 0)
-            transpose_in(r, 1)
-            if r == 0:
-                quantise(0)
+        transpose_in(0, 0)
+        transpose_in(0, 1)
+        spread_first()
+        quantise(0)
+        transpose_in(1, 0)
+        transpose_in(1, 1)
         for r in range(ROUNDS + OUT_LAG):
             if r + 1 < ROUNDS:
                 quantise(r + 1)
             if r < ROUNDS:
                 for c in range(FEATURE_BLOCKS):
                     multiply(r, c)
+                if r == 0:
+                    spread_second()
+                for c in range(FEATURE_BLOCKS):
                     normalise(r, c)
             if r + IN_LEAD < ROUNDS:
                 transpose_in(r + IN_LEAD, 0)

import concourse.mybir as mybir
from concourse.masks import make_identity

F32 = mybir.dt.float32
BF16 = mybir.dt.bfloat16
I32 = mybir.dt.int32
U32 = mybir.dt.uint32
U8 = mybir.dt.uint8
FP8X4 = mybir.dt.float8_e4m3fn_x4
ACT = mybir.ActivationFunctionType
ALU = mybir.AluOpType

P = 128
ROWS = 4096
K = 512
FEATURES = 512
EXPERTS = 3
EPS = 1e-5

CHUNK = 512
ROW_BLOCKS = CHUNK // P
FEATURE_BLOCKS = FEATURES // P
CHUNKS = ROWS // CHUNK
ROUNDS = CHUNKS * EXPERTS
WORDS = K // 2
COLUMNS = EXPERTS * FEATURE_BLOCKS
OUT_LAG = 1
IN_LEAD = 2
OUT_BUFS = 3
AHEAD = 12

FLOPS = 2 * ROWS * K * FEATURES * EXPERTS


def tile_mom_t_e_kernel(
    tc, x1, x2, x3, W_words, W_scales, b, gamma, beta, running_mean, running_var, out
):
    nc = tc.nc
    xs = [x1, x2, x3]

    with tc.tile_pool(name="keep", bufs=1) as keep, tc.tile_pool(
        name="rows_in", bufs=1
    ) as rows_in, tc.tile_pool(name="quantised", bufs=IN_LEAD + 1) as quantised, tc.tile_pool(
        name="features_first", bufs=(OUT_LAG + 1) * FEATURE_BLOCKS
    ) as features_first, tc.tile_pool(name="rows_out", bufs=OUT_BUFS) as rows_out, tc.psum_pool(name="psum", bufs=8) as psum, tc.manual_schedule():
        x_rows = []
        for r in range(ROUNDS):
            x_rows.append(rows_in.tile([P, ROW_BLOCKS, K], BF16, name="x_rows%d" % r))

        def load_rows(r):
            chunk, e = divmod(r, EXPERTS)
            nc.sync.dma_start(
                out=x_rows[r][:],
                in_=xs[e][chunk * CHUNK : (chunk + 1) * CHUNK, :].rearrange(
                    "(p j) k -> p j k", j=ROW_BLOCKS
                ),
            )

        load_rows(0)
        load_rows(1)

        first_rows = keep.tile([P, P], BF16)
        nc.vector.memset(first_rows[:], 0.0)
        second_rows = keep.tile([P, P], BF16)
        nc.vector.memset(second_rows[:], 0.0)
        ident = keep.tile([P, P], F32)
        make_identity(nc, ident[:])
        for rows_tile, vectors in (
            (first_rows, [running_var, b]),
            (second_rows, [gamma, beta, running_mean]),
        ):
            for v, vec in enumerate(vectors):
                nc.gpsimd.dma_start(
                    out=rows_tile[v * COLUMNS : (v + 1) * COLUMNS, :],
                    in_=vec.rearrange("o e (c f) -> (o e c) f", f=P),
                )
        warm = keep.tile([P, 2], F32)
        nc.vector.memset(warm[:], 1.0)
        nc.scalar.sqrt(out=warm[:, 1:2], in_=warm[:, 0:1])

        w_scales = keep.tile([P, EXPERTS, FEATURES], U8, align_bytes=64)
        nc.vector.memset(w_scales[:].rearrange("p g n -> p (g n)").bitcast(I32), 0)
        for quadrant in range(4):
            nc.sync.dma_start(
                out=w_scales[32 * quadrant : 32 * quadrant + 4, :, :].bitcast(I32),
                in_=W_scales[:, 4 * quadrant : 4 * quadrant + 4, :]
                .rearrange("g r n -> r g n")
                .bitcast(I32),
            )
        w_codes = keep.tile([P, EXPERTS, FEATURES], U32, align_bytes=64)
        for e in range(EXPERTS):
            nc.sync.dma_start(
                out=w_codes[:, e, :].bitcast(I32),
                in_=W_words[e].rearrange("p n t -> p (n t)").bitcast(I32),
            )
            load_rows(IN_LEAD + e)
        for r in range(IN_LEAD + EXPERTS, AHEAD):
            load_rows(r)

        first_cols = keep.tile([P, 2, COLUMNS], F32)
        bias = first_cols[:, 1, :]
        second_cols = keep.tile([P, 3, COLUMNS], F32)
        gain = keep.tile([P, COLUMNS], F32)
        shift = keep.tile([P, COLUMNS], F32)

        def spread_first():
            first_f32 = keep.tile([P, P], F32)
            nc.scalar.copy(out=first_f32[:], in_=first_rows[:])
            first_psum = psum.tile([P, P], F32, tag="bank")
            nc.tensor.transpose(first_psum[:], first_f32[:], ident[:])
            nc.scalar.copy(
                out=first_cols[:].rearrange("p v c -> p (v c)"), in_=first_psum[:, : 2 * COLUMNS]
            )
            nc.vector.tensor_scalar_add(out=gain[:], in0=first_cols[:, 0, :], scalar1=EPS)
            nc.scalar.sqrt(out=gain[:], in_=gain[:])
            nc.scalar.activation(out=warm[:, 1:2], in_=warm[:, 0:1], func=ACT.Gelu_apprx_sigmoid)

        def spread_second():
            second_f32 = keep.tile([P, P], F32)
            nc.vector.tensor_copy(out=second_f32[:], in_=second_rows[:])
            second_psum = psum.tile([P, P], F32, tag="bank")
            nc.tensor.transpose(second_psum[:], second_f32[:], ident[:])
            nc.vector.tensor_copy(
                out=second_cols[:].rearrange("p v c -> p (v c)"), in_=second_psum[:, : 3 * COLUMNS]
            )
            nc.vector.reciprocal(out=gain[:], in_=gain[:])
            nc.vector.tensor_mul(out=gain[:], in0=gain[:], in1=second_cols[:, 0, :])
            nc.vector.tensor_mul(out=shift[:], in0=gain[:], in1=second_cols[:, 2, :])
            nc.vector.tensor_sub(out=shift[:], in0=second_cols[:, 1, :], in1=shift[:])

        grouped = {}
        x_codes = {}
        x_scales = {}
        finished = {}
        out_rows = {}

        def transpose_in(r, half):
            if half == 0:
                grouped[r] = quantised.tile([P, CHUNK * 4], BF16, name="grouped", align_bytes=64)
            words = x_rows[r][:].rearrange("p j k -> p (j k)").bitcast(F32)
            pairs = grouped[r][:].bitcast(F32).rearrange("p (n u) -> p n u", u=2)
            x_psum = psum.tile([P, 2, CHUNK // 2], F32, tag="bank")
            for jj in range(ROW_BLOCKS // 2):
                j = half * (ROW_BLOCKS // 2) + jj
                for u in range(2):
                    nc.tensor.transpose(
                        x_psum[:, u, jj * P : (jj + 1) * P],
                        words[:, j * WORDS + u : (j + 1) * WORDS : 2],
                        ident[:],
                    )
            nc.vector.tensor_copy(
                out=pairs[:, half * (CHUNK // 2) : (half + 1) * (CHUNK // 2), :],
                in_=x_psum[:].rearrange("p u n -> p n u"),
            )

        def quantise(r):
            x_codes[r] = quantised.tile([P, CHUNK], U32, name="x_codes", align_bytes=64)
            x_scales[r] = quantised.tile([P, CHUNK], U8, name="x_scales", align_bytes=64)
            nc.vector.quantize_mx(
                out=x_codes[r][:].bitcast(FP8X4), scales=x_scales[r][:], in_=grouped[r][:]
            )

        def multiply(r, c):
            e = r % EXPERTS
            cols = slice(c * P, (c + 1) * P)
            col = slice(e * FEATURE_BLOCKS + c, e * FEATURE_BLOCKS + c + 1)
            acc = psum.tile([P, CHUNK], F32, tag="bank")
            nc.tensor.matmul_mx(
                out=acc[:],
                lhsT=w_codes[:, e, cols].bitcast(FP8X4),
                lhsT_scale=w_scales[:, e, cols],
                rhs=x_codes[r][:].bitcast(FP8X4),
                rhs_scale=x_scales[r][:],
                start=True,
                stop=True,
            )
            z = features_first.tile([P, CHUNK], F32, name="z")
            nc.scalar.activation(
                out=z[:], in_=acc[:], func=ACT.Gelu_apprx_sigmoid, bias=bias[:, col], scale=1.0
            )
            finished[(r, c)] = z

        def normalise(r, c):
            col = slice((r % EXPERTS) * FEATURE_BLOCKS + c, (r % EXPERTS) * FEATURE_BLOCKS + c + 1)
            z = finished[(r, c)]
            if c < FEATURE_BLOCKS - 1:
                nc.gpsimd.tensor_scalar(
                    out=z[:],
                    in0=z[:],
                    scalar1=gain[:, col],
                    scalar2=shift[:, col],
                    op0=ALU.mult,
                    op1=ALU.add,
                )
            else:
                nc.scalar.activation(
                    out=z[:], in_=z[:], func=ACT.Identity, bias=shift[:, col], scale=gain[:, col]
                )

        def transpose_out(r, c):
            chunk, e = divmod(r, EXPERTS)
            if c == 0 and e == 0:
                out_rows[chunk] = rows_out.tile(
                    [P, ROW_BLOCKS, EXPERTS * FEATURES], F32, name="out_rows"
                )
            o_psum = psum.tile([P, ROW_BLOCKS, P], F32, tag="bank")
            for j in range(ROW_BLOCKS):
                nc.tensor.transpose(
                    o_psum[:, j, :], finished[(r, c)][:, j * P : (j + 1) * P], ident[:]
                )
            target = out_rows[chunk][:, :, e * FEATURES + c * P : e * FEATURES + (c + 1) * P]
            if r == ROUNDS - 1:
                on_vector = c % 2 == 0
            elif r + OUT_LAG + IN_LEAD >= ROUNDS:
                on_vector = True
            else:
                on_vector = c != 1
            if on_vector:
                nc.vector.tensor_copy(out=target, in_=o_psum[:])
            else:
                nc.scalar.copy(out=target, in_=o_psum[:])
            if c == FEATURE_BLOCKS - 1:
                rows = out[chunk * CHUNK : (chunk + 1) * CHUNK, :].rearrange(
                    "(p j) f -> p j f", j=ROW_BLOCKS
                )
                if chunk >= CHUNKS - 2:
                    cols = slice(e * FEATURES, (e + 1) * FEATURES)
                    nc.sync.dma_start(out=rows[:, :, cols], in_=out_rows[chunk][:, :, cols])
                elif e == EXPERTS - 1:
                    nc.sync.dma_start(out=rows, in_=out_rows[chunk][:])
                    for later in range(r + 1 + AHEAD - EXPERTS, r + 1 + AHEAD):
                        if later < ROUNDS:
                            load_rows(later)

        transpose_in(0, 0)
        transpose_in(0, 1)
        spread_first()
        quantise(0)
        transpose_in(1, 0)
        transpose_in(1, 1)
        for r in range(ROUNDS + OUT_LAG):
            if r + 1 < ROUNDS:
                quantise(r + 1)
            if r < ROUNDS:
                for c in range(FEATURE_BLOCKS):
                    multiply(r, c)
                if r == 0:
                    spread_second()
                for c in range(FEATURE_BLOCKS):
                    normalise(r, c)
            if r + IN_LEAD < ROUNDS:
                transpose_in(r + IN_LEAD, 0)
                transpose_in(r + IN_LEAD, 1)
            if r >= OUT_LAG:
                for c in range(FEATURE_BLOCKS):
                    transpose_out(r - OUT_LAG, c)
